import numpy as np
import ml_dtypes


def mxq(x, axis, fmt="e4m3"):
    dtype, down = {"e4m3": (ml_dtypes.float8_e4m3fn, 7), "e5m2": (ml_dtypes.float8_e5m2, 14)}[fmt]
    v = np.moveaxis(np.asarray(x, np.float32).astype(ml_dtypes.bfloat16).astype(np.float64), axis, -1)
    blocks = v.reshape(v.shape[:-1] + (-1, 32))
    amax = np.abs(blocks).max(-1, keepdims=True)
    byte = np.maximum(np.where(amax > 0, np.frexp(amax)[1] - 1 + 127, 0) - down, 1)
    scale = np.exp2(byte - 127.0)
    codes = (blocks / scale).astype(np.float32).astype(dtype).astype(np.float64)
    return np.moveaxis((codes * scale).reshape(v.shape), -1, axis)


WIDE = False


def mx_kscale(k):
    if not WIDE:
        return np.ones(k)
    levels = np.array([10, -10, 5, -5, 0])
    a = np.random.permutation(np.resize(levels, k // 512 * 4)).reshape(k // 512, 4)
    idx = np.arange(k)
    return np.exp2(a[idx // 512, idx % 128 // 32])


BF16 = ml_dtypes.bfloat16


def bf(x):
    return np.asarray(x, np.float32).astype(BF16)


def f64(x):
    return np.asarray(x).astype(np.float64)


B, S, H, D = 1, 1024, 16, 128


def setup_inputs():
    s = mx_kscale(S)
    return {"query": bf(np.random.standard_normal((B, S, H * D)) * 1.5),
            "key": bf(np.random.standard_normal((B, S, H * D))),
            "value": bf(np.random.standard_normal((B, S, H * D)) * 2.0 * (s.max() / s)[None, :, None]),
            "attention_mask": bf(np.random.standard_normal((1, 1, S, S)) * 0.5 + np.log(s)[None, None, None, :])}


def reference(query, key, value, attention_mask):
    q = f64(query).reshape(B, S, H, D).transpose(0, 2, 1, 3)
    k = f64(key).reshape(B, S, H, D).transpose(0, 2, 1, 3)
    v = f64(value).reshape(B, S, H, D).transpose(0, 2, 1, 3)
    scores = q @ k.transpose(0, 1, 3, 2) / np.sqrt(D)
    scores = scores + f64(attention_mask)
    e = np.exp(scores - scores.max(-1, keepdims=True))
    out = (mxq(e, 3, "e4m3") @ mxq(v, 2, "e4m3")) / e.sum(-1, keepdims=True)
    return out.transpose(0, 2, 1, 3).reshape(B, S, H * D)

@@ -1,0 +1,219 @@
+import math
+from contextlib import ExitStack
+
+import concourse.mybir as mybir
+from concourse.masks import make_identity
+
+F32 = mybir.dt.float32
+BF16 = mybir.dt.bfloat16
+U32 = mybir.dt.uint32
+U8 = mybir.dt.uint8
+FP8X4 = mybir.dt.float8_e4m3fn_x4
+ALU = mybir.AluOpType
+ACT = mybir.ActivationFunctionType
+AX = mybir.AxisListType
+
+P = 128
+S = 1024
+H = 16
+D = 128
+NT = S // P
+HB = 4
+CB = HB * D
+FLOPS = 2 * 2 * H * S * S * D
+SQRT_D = math.sqrt(float(D))
+SCALE = 1.0 / SQRT_D
+
+MASK_ON_PE = True
+REGROUP_ON_POOL = True
+
+
+def tile_flashattention_kernel(tc, query, key, value, attention_mask, out):
+    nc = tc.nc
+    q_v = query.rearrange("b (i p) c -> p (b i) c", p=P)
+    k_v = key.rearrange("b (i p) c -> p (b i) c", p=P)
+    v_v = value.rearrange("b (i p) c -> p (b i) c", p=P)
+    m_v = attention_mask.rearrange("a b (i p) k -> p (a b i) k", p=P)
+    o_v = out.rearrange("b (i p) c -> p (b i) c", p=P)
+
+    with ExitStack() as ctx:
+        const = ctx.enter_context(tc.tile_pool(name="const", bufs=1))
+        raw = ctx.enter_context(tc.tile_pool(name="raw", bufs=2))
+        hp = ctx.enter_context(tc.tile_pool(name="hp", bufs=2))
+        work = ctx.enter_context(tc.tile_pool(name="work", bufs=3))
+        stat = ctx.enter_context(tc.tile_pool(name="stat", bufs=4))
+        ps_sc = ctx.enter_context(tc.psum_pool(name="ps_sc", bufs=4))
+        ps_tr = ctx.enter_context(tc.psum_pool(name="ps_tr", bufs=2))
+        ps_o = ctx.enter_context(tc.psum_pool(name="ps_o", bufs=2))
+
+        ident_bf = const.tile([P, P], BF16)
+        make_identity(nc, ident_bf[:])
+        ident_f = const.tile([P, P], F32)
+        make_identity(nc, ident_f[:])
+        m_raw = const.tile([P, NT, S], BF16)
+        mask_t = const.tile([P, NT, NT, P], F32)
+
+        blocks = {}
+        heads = {}
+
+        def load_block(cb):
+            cols = slice(cb * CB, (cb + 1) * CB)
+            kr = raw.tile([P, NT, CB], BF16, tag="kr")
+            nc.sync.dma_start(out=kr[:], in_=k_v[:, :, cols])
+            qr = raw.tile([P, NT, CB], BF16, tag="qr")
+            nc.sync.dma_start(out=qr[:], in_=q_v[:, :, cols])
+            blocks[cb] = (qr, kr)
+
+        def load_values(cb):
+            cols = slice(cb * CB, (cb + 1) * CB)
+            vr = raw.tile([P, NT, CB], BF16, tag="vr")
+            nc.sync.dma_start(out=vr[:], in_=v_v[:, :, cols])
+            blocks[(cb, "v")] = vr
+
+        def load_mask(i0, i1):
+            nc.sync.dma_start(out=m_raw[:, i0:i1, :], in_=m_v[:, i0:i1, :])
+
+        def mask_prep(i):
+            tm = ps_tr.tile([P, NT, P], BF16, tag="tr")
+            for j in range(NT):
+                nc.tensor.transpose(tm[:, j, :], m_raw[:, i, j * P:(j + 1) * P], ident_bf[:])
+            nc.scalar.activation(out=mask_t[:, i], in_=tm[:], func=ACT.Copy, scale=SQRT_D)
+
+        def head_prep(h):
+            cb, hc = divmod(h, HB)
+            qr, kr = blocks[cb]
+            vr = blocks[(cb, "v")]
+            cols = slice(hc * D, (hc + 1) * D)
+            tk = ps_tr.tile([P, NT, P], BF16, tag="tr")
+            for j in range(NT):
+                nc.tensor.transpose(tk[:, j, :], kr[:, j, cols], ident_bf[:])
+            k_t = hp.tile([P, S], BF16, tag="k_t")
+            nc.vector.tensor_copy(out=k_t[:], in_=tk[:].rearrange("p j q -> p (j q)"))
+            tq = ps_tr.tile([P, NT, P], BF16, tag="tr")
+            for j in range(NT):
+                nc.tensor.transpose(tq[:, j, :], qr[:, j, cols], ident_bf[:])
+            q_t = hp.tile([P, S], BF16, tag="q_t")
+            nc.scalar.copy(out=q_t[:], in_=tq[:].rearrange("p j q -> p (j q)"))
+            gv = hp.tile([P, 2, D, 4], BF16, tag="gv", align_bytes=64)
+            v_src = vr[:, :, cols].rearrange("p (g t) c -> p g c t", g=2)
+            if REGROUP_ON_POOL and h > 0:
+                nc.gpsimd.tensor_scalar(out=gv[:], in0=v_src, scalar1=1.0, scalar2=0.0, op0=ALU.mult, op1=ALU.add)
+            else:
+                nc.vector.tensor_copy(out=gv[:], in_=v_src)
+            vc = hp.tile([P, 2 * D], U32, tag="vc", align_bytes=64)
+            vs = hp.tile([P, 2 * D], U8, tag="vs", align_bytes=64)
+            nc.vector.quantize_mx(
+                out=vc[:].bitcast(FP8X4), scales=vs[:], in_=gv[:].rearrange("p g c t -> p (g c t)")
+            )
+            heads[h] = (q_t, k_t, vc, vs)
+
+        group = {}
+
+        def unit(h, i):
+            n = h * NT + i
+            u = i % 4
+            q_t, k_t, vc, vs = heads[h]
+            if u == 0:
+                po_new = ps_o.tile([P, 4, D], F32, tag="po")
+                rs_new = stat.tile([P, 4, 2], F32, tag="rs")
+                group["po"] = po_new
+                group["rs"] = rs_new
+            po = group["po"]
+            rs = group["rs"]
+
+            sc = []
+            for c in range(2):
+                sc_c = ps_sc.tile([P, 512], F32, tag="sc")
+                sc.append(sc_c)
+                nc.tensor.matmul(
+                    sc_c[:], lhsT=q_t[:, i * P:(i + 1) * P], rhs=k_t[:, c * 512:(c + 1) * 512],
+                    start=True, stop=not MASK_ON_PE,
+                )
+                if MASK_ON_PE:
+                    for jj in range(4):
+                        nc.tensor.matmul(
+                            sc_c[:, jj * P:(jj + 1) * P], lhsT=mask_t[:, i, 4 * c + jj, :], rhs=ident_f[:],
+                            is_transpose=True, start=False, stop=(jj == 3),
+                        )
+
+            mx = stat.tile([P, 2], F32, tag="mx")
+            nb = stat.tile([P, 1], F32, tag="nb")
+            e = work.tile([P, S], BF16, tag="e")
+            if MASK_ON_PE:
+                for c in range(2):
+                    nc.vector.reduce_max(out=mx[:, c:c + 1], in_=sc[c][:], axis=AX.X)
+                nc.vector.tensor_scalar(
+                    out=nb[:], in0=mx[:, 0:1], scalar1=mx[:, 1:2], scalar2=-SCALE, op0=ALU.max, op1=ALU.mult
+                )
+                for c in range(2):
+                    nc.scalar.activation(
+                        out=e[:, c * 512:(c + 1) * 512], in_=sc[c][:], func=ACT.Exp,
+                        bias=nb[:], scale=SCALE, accum_out=rs[:, u, c:c + 1],
+                    )
+            else:
+                t = work.tile([P, S], F32, tag="t")
+                for c in range(2):
+                    nc.vector.scalar_tensor_tensor(
+                        out=t[:, c * 512:(c + 1) * 512], in0=sc[c][:], scalar=SCALE,
+                        in1=m_raw[:, i, c * 512:(c + 1) * 512], op0=ALU.mult, op1=ALU.add,
+                    )
+                nc.vector.reduce_max(out=mx[:, 0:1], in_=t[:], axis=AX.X)
+                nc.vector.tensor_scalar(
+                    out=nb[:], in0=mx[:, 0:1], scalar1=-1.0, scalar2=None, op0=ALU.mult
+                )
+                for c in range(2):
+                    nc.scalar.activation(
+                        out=e[:, c * 512:(c + 1) * 512], in_=t[:, c * 512:(c + 1) * 512], func=ACT.Exp,
+                        bias=nb[:], scale=1.0, accum_out=rs[:, u, c:c + 1],
+                    )
+
+            te = ps_tr.tile([P, NT, P], BF16, tag="tr")
+            for b in range(NT):
+                nc.tensor.transpose(te[:, b, :], e[:, b * P:(b + 1) * P], ident_bf[:])
+            gr = work.tile([P, 2, P, 4], BF16, tag="gr", align_bytes=64)
+            te_v = te[:].rearrange("p (g t) q -> p g q t", g=2)
+            if n % 2 == 0:
+                nc.vector.tensor_copy(out=gr[:], in_=te_v)
+            else:
+                nc.scalar.copy(out=gr[:], in_=te_v)
+            cd = work.tile([P, 2 * P], U32, tag="cd", align_bytes=64)
+            sl = work.tile([P, 2 * P], U8, tag="sl", align_bytes=64)
+            nc.vector.quantize_mx(
+                out=cd[:].bitcast(FP8X4), scales=sl[:], in_=gr[:].rearrange("p g q t -> p (g q t)")
+            )
+            for g in range(2):
+                nc.tensor.matmul_mx(
+                    out=po[:, u, :],
+                    lhsT=cd[:, g * P:(g + 1) * P].bitcast(FP8X4), lhsT_scale=sl[:, g * P:(g + 1) * P],
+                    rhs=vc[:, g * D:(g + 1) * D].bitcast(FP8X4), rhs_scale=vs[:, g * D:(g + 1) * D],
+                    start=(g == 0), stop=(g == 1),
+                )
+
+            if u == 3:
+                rsum = stat.tile([P, 4], F32, tag="rsum")
+                nc.vector.reduce_sum(out=rsum[:], in_=rs[:], axis=AX.X)
+                rc = stat.tile([P, 4], F32, tag="rc")
+                nc.vector.reciprocal(out=rc[:], in_=rsum[:])
+                osb = work.tile([P, 4, D], F32, tag="osb")
+                for w in range(4):
+                    nc.scalar.activation(out=osb[:, w, :], in_=po[:, w, :], func=ACT.Copy, scale=rc[:, w:w + 1])
+                nc.sync.dma_start(out=o_v[:, i - 3:i + 1, h * D:(h + 1) * D], in_=osb[:])
+
+        load_block(0)
+        load_mask(0, 2)
+        load_values(0)
+        load_mask(2, 4)
+        load_mask(4, 8)
+        load_block(1)
+        load_values(1)
+        head_prep(0)
+        for h in range(H):
+            for i in range(NT):
+                if h == 0 and MASK_ON_PE:
+                    mask_prep(i)
+                unit(h, i)
+                if i == 0 and h % HB == 0 and 0 < h and h // HB + 1 < H // HB:
+                    load_block(h // HB + 1)
+                    load_values(h // HB + 1)
+                if i == 2 and h + 1 < H:
+                    head_prep(h + 1)

@@ -11,7 +11,6 @@ U8 = mybir.dt.uint8
 FP8X4 = mybir.dt.float8_e4m3fn_x4
 ALU = mybir.AluOpType
 ACT = mybir.ActivationFunctionType
-AX = mybir.AxisListType
 
 P = 128
 S = 1024
@@ -20,12 +19,13 @@ D = 128
 NT = S // P
 HB = 4
 CB = HB * D
+N_UNITS = H * NT
 FLOPS = 2 * 2 * H * S * S * D
 SQRT_D = math.sqrt(float(D))
 SCALE = 1.0 / SQRT_D
 
-MASK_ON_PE = True
-REGROUP_ON_POOL = True
+PINNED = True
+E_ON_VECTOR_EVERY = 0
 
 
 def tile_flashattention_kernel(tc, query, key, value, attention_mask, out):
@@ -37,6 +37,8 @@ def tile_flashattention_kernel(tc, query, key, value, attention_mask, out):
     o_v = out.rearrange("b (i p) c -> p (b i) c", p=P)
 
     with ExitStack() as ctx:
+        if PINNED:
+            ctx.enter_context(tc.manual_schedule())
         const = ctx.enter_context(tc.tile_pool(name="const", bufs=1))
         raw = ctx.enter_context(tc.tile_pool(name="raw", bufs=2))
         hp = ctx.enter_context(tc.tile_pool(name="hp", bufs=2))
@@ -55,6 +57,7 @@ def tile_flashattention_kernel(tc, query, key, value, attention_mask, out):
 
         blocks = {}
         heads = {}
+        st = {}
 
         def load_block(cb):
             cols = slice(cb * CB, (cb + 1) * CB)
@@ -62,125 +65,135 @@ def tile_flashattention_kernel(tc, query, key, value, attention_mask, out):
             nc.sync.dma_start(out=kr[:], in_=k_v[:, :, cols])
             qr = raw.tile([P, NT, CB], BF16, tag="qr")
             nc.sync.dma_start(out=qr[:], in_=q_v[:, :, cols])
-            blocks[cb] = (qr, kr)
-
-        def load_values(cb):
-            cols = slice(cb * CB, (cb + 1) * CB)
             vr = raw.tile([P, NT, CB], BF16, tag="vr")
             nc.sync.dma_start(out=vr[:], in_=v_v[:, :, cols])
-            blocks[(cb, "v")] = vr
-
-        def load_mask(i0, i1):
-            nc.sync.dma_start(out=m_raw[:, i0:i1, :], in_=m_v[:, i0:i1, :])
+            blocks[cb] = (qr, kr, vr)
 
         def mask_prep(i):
-            tm = ps_tr.tile([P, NT, P], BF16, tag="tr")
+            tm = ps_sc.tile([P, NT, P], BF16, tag="sc")
             for j in range(NT):
                 nc.tensor.transpose(tm[:, j, :], m_raw[:, i, j * P:(j + 1) * P], ident_bf[:])
-            nc.scalar.activation(out=mask_t[:, i], in_=tm[:], func=ACT.Copy, scale=SQRT_D)
+            if i % 2 == 0:
+                nc.scalar.activation(out=mask_t[:, i], in_=tm[:], func=ACT.Copy, scale=SQRT_D)
+            else:
+                nc.vector.tensor_scalar(out=mask_t[:, i], in0=tm[:], scalar1=SQRT_D, scalar2=None, op0=ALU.mult)
 
-        def head_prep(h):
+        def prep_transposes(h, which):
             cb, hc = divmod(h, HB)
-            qr, kr = blocks[cb]
-            vr = blocks[(cb, "v")]
-            cols = slice(hc * D, (hc + 1) * D)
-            tk = ps_tr.tile([P, NT, P], BF16, tag="tr")
+            src = blocks[cb][which]
+            tp = ps_sc.tile([P, NT, P], BF16, tag="sc")
             for j in range(NT):
-                nc.tensor.transpose(tk[:, j, :], kr[:, j, cols], ident_bf[:])
-            k_t = hp.tile([P, S], BF16, tag="k_t")
-            nc.vector.tensor_copy(out=k_t[:], in_=tk[:].rearrange("p j q -> p (j q)"))
-            tq = ps_tr.tile([P, NT, P], BF16, tag="tr")
-            for j in range(NT):
-                nc.tensor.transpose(tq[:, j, :], qr[:, j, cols], ident_bf[:])
-            q_t = hp.tile([P, S], BF16, tag="q_t")
-            nc.scalar.copy(out=q_t[:], in_=tq[:].rearrange("p j q -> p (j q)"))
+                nc.tensor.transpose(tp[:, j, :], src[:, j, hc * D:(hc + 1) * D], ident_bf[:])
+            st[("tp", h, which)] = tp
+
+        def prep_copy(h, which):
+            tp = st[("tp", h, which)]
+            x_t = hp.tile([P, S], BF16, tag="x_t%d" % which)
+            nc.vector.tensor_copy(out=x_t[:], in_=tp[:].rearrange("p j q -> p (j q)"))
+            heads[(h, which)] = x_t
+
+        def prep_regroup(h, on_pool):
+            cb, hc = divmod(h, HB)
+            vr = blocks[cb][2]
             gv = hp.tile([P, 2, D, 4], BF16, tag="gv", align_bytes=64)
-            v_src = vr[:, :, cols].rearrange("p (g t) c -> p g c t", g=2)
-            if REGROUP_ON_POOL and h > 0:
+            v_src = vr[:, :, hc * D:(hc + 1) * D].rearrange("p (g t) c -> p g c t", g=2)
+            if on_pool:
                 nc.gpsimd.tensor_scalar(out=gv[:], in0=v_src, scalar1=1.0, scalar2=0.0, op0=ALU.mult, op1=ALU.add)
             else:
                 nc.vector.tensor_copy(out=gv[:], in_=v_src)
+            st[("gv", h)] = gv
+
+        def prep_quantise(h):
+            gv = st[("gv", h)]
             vc = hp.tile([P, 2 * D], U32, tag="vc", align_bytes=64)
             vs = hp.tile([P, 2 * D], U8, tag="vs", align_bytes=64)
             nc.vector.quantize_mx(
                 out=vc[:].bitcast(FP8X4), scales=vs[:], in_=gv[:].rearrange("p g c t -> p (g c t)")
             )
-            heads[h] = (q_t, k_t, vc, vs)
+            heads[(h, 2)] = (vc, vs)
 
-        group = {}
-
-        def unit(h, i):
-            n = h * NT + i
-            u = i % 4
-            q_t, k_t, vc, vs = heads[h]
-            if u == 0:
-                po_new = ps_o.tile([P, 4, D], F32, tag="po")
-                rs_new = stat.tile([P, 4, 2], F32, tag="rs")
-                group["po"] = po_new
-                group["rs"] = rs_new
-            po = group["po"]
-            rs = group["rs"]
-
-            sc = []
+        def stage_a(n):
+            h, i = divmod(n, NT)
+            q_t = heads[(h, 0)]
+            k_t = heads[(h, 1)]
             for c in range(2):
                 sc_c = ps_sc.tile([P, 512], F32, tag="sc")
-                sc.append(sc_c)
+                st[("sc", n, c)] = sc_c
                 nc.tensor.matmul(
                     sc_c[:], lhsT=q_t[:, i * P:(i + 1) * P], rhs=k_t[:, c * 512:(c + 1) * 512],
-                    start=True, stop=not MASK_ON_PE,
+                    start=True, stop=False,
                 )
-                if MASK_ON_PE:
-                    for jj in range(4):
-                        nc.tensor.matmul(
-                            sc_c[:, jj * P:(jj + 1) * P], lhsT=mask_t[:, i, 4 * c + jj, :], rhs=ident_f[:],
-                            is_transpose=True, start=False, stop=(jj == 3),
-                        )
-
-            mx = stat.tile([P, 2], F32, tag="mx")
-            nb = stat.tile([P, 1], F32, tag="nb")
-            e = work.tile([P, S], BF16, tag="e")
-            if MASK_ON_PE:
-                for c in range(2):
-                    nc.vector.reduce_max(out=mx[:, c:c + 1], in_=sc[c][:], axis=AX.X)
-                nc.vector.tensor_scalar(
-                    out=nb[:], in0=mx[:, 0:1], scalar1=mx[:, 1:2], scalar2=-SCALE, op0=ALU.max, op1=ALU.mult
-                )
-                for c in range(2):
-                    nc.scalar.activation(
-                        out=e[:, c * 512:(c + 1) * 512], in_=sc[c][:], func=ACT.Exp,
-                        bias=nb[:], scale=SCALE, accum_out=rs[:, u, c:c + 1],
+                for jj in range(4):
+                    nc.tensor.matmul(
+                        sc_c[:, jj * P:(jj + 1) * P], lhsT=mask_t[:, i, 4 * c + jj, :], rhs=ident_f[:],
+                        is_transpose=True, start=False, stop=(jj == 3),
                     )
+
+        def stage_b(n, c):
+            if c == 0:
+                t_new = work.tile([P, S], F32, tag="t")
+                st[("t", n)] = t_new
+                nb0_new = stat.tile([P, 1], F32, tag="nb0")
+                st[("nb", n, 0)] = nb0_new
             else:
-                t = work.tile([P, S], F32, tag="t")
-                for c in range(2):
-                    nc.vector.scalar_tensor_tensor(
-                        out=t[:, c * 512:(c + 1) * 512], in0=sc[c][:], scalar=SCALE,
-                        in1=m_raw[:, i, c * 512:(c + 1) * 512], op0=ALU.mult, op1=ALU.add,
-                    )
-                nc.vector.reduce_max(out=mx[:, 0:1], in_=t[:], axis=AX.X)
-                nc.vector.tensor_scalar(
-                    out=nb[:], in0=mx[:, 0:1], scalar1=-1.0, scalar2=None, op0=ALU.mult
-                )
-                for c in range(2):
-                    nc.scalar.activation(
-                        out=e[:, c * 512:(c + 1) * 512], in_=t[:, c * 512:(c + 1) * 512], func=ACT.Exp,
-                        bias=nb[:], scale=1.0, accum_out=rs[:, u, c:c + 1],
-                    )
+                nb1_new = stat.tile([P, 1], F32, tag="nb1")
+                st[("nb", n, 1)] = nb1_new
+            t = st[("t", n)]
+            nc.vector.tensor_scalar(
+                out=t[:, c * 512:(c + 1) * 512], in0=st[("sc", n, c)][:], scalar1=-SCALE,
+                scalar2=(None if c == 0 else st[("nb", n, 0)][:]), op0=ALU.mult, op1=ALU.min,
+                accum_out=st[("nb", n, c)][:],
+            )
 
+        def stage_c(n):
+            u = n % 4
+            if u == 0:
+                rs_new = stat.tile([P, 4], F32, tag="rs")
+                st[("rs", n // 4)] = rs_new
+            rs = st[("rs", n // 4)]
+            e = work.tile([P, S], BF16, tag="e")
+            st[("e", n)] = e
+            nc.scalar.activation(
+                out=e[:], in_=st[("t", n)][:], func=ACT.Exp, bias=st[("nb", n, 1)][:], scale=-1.0,
+                accum_out=rs[:, u:u + 1],
+            )
+
+        def stage_d(n):
+            e = st[("e", n)]
             te = ps_tr.tile([P, NT, P], BF16, tag="tr")
+            st[("te", n)] = te
             for b in range(NT):
                 nc.tensor.transpose(te[:, b, :], e[:, b * P:(b + 1) * P], ident_bf[:])
+
+        def e_on_vector(n):
+            return E_ON_VECTOR_EVERY > 0 and n % E_ON_VECTOR_EVERY == E_ON_VECTOR_EVERY - 1
+
+        def stage_e(n):
             gr = work.tile([P, 2, P, 4], BF16, tag="gr", align_bytes=64)
-            te_v = te[:].rearrange("p (g t) q -> p g q t", g=2)
-            if n % 2 == 0:
+            st[("gr", n)] = gr
+            te_v = st[("te", n)][:].rearrange("p (g t) q -> p g q t", g=2)
+            if e_on_vector(n):
                 nc.vector.tensor_copy(out=gr[:], in_=te_v)
             else:
                 nc.scalar.copy(out=gr[:], in_=te_v)
+
+        def stage_f(n):
             cd = work.tile([P, 2 * P], U32, tag="cd", align_bytes=64)
             sl = work.tile([P, 2 * P], U8, tag="sl", align_bytes=64)
+            st[("cd", n)] = (cd, sl)
             nc.vector.quantize_mx(
-                out=cd[:].bitcast(FP8X4), scales=sl[:], in_=gr[:].rearrange("p g q t -> p (g q t)")
+                out=cd[:].bitcast(FP8X4), scales=sl[:], in_=st[("gr", n)][:].rearrange("p g q t -> p (g q t)")
             )
+
+        def stage_g(n):
+            h = n // NT
+            u = n % 4
+            if u == 0:
+                po_new = ps_o.tile([P, 4, D], F32, tag="po")
+                st[("po", n // 4)] = po_new
+            po = st[("po", n // 4)]
+            cd, sl = st[("cd", n)]
+            vc, vs = heads[(h, 2)]
             for g in range(2):
                 nc.tensor.matmul_mx(
                     out=po[:, u, :],
@@ -189,31 +202,59 @@ def tile_flashattention_kernel(tc, query, key, value, attention_mask, out):
                     start=(g == 0), stop=(g == 1),
                 )
 
-            if u == 3:
-                rsum = stat.tile([P, 4], F32, tag="rsum")
-                nc.vector.reduce_sum(out=rsum[:], in_=rs[:], axis=AX.X)
-                rc = stat.tile([P, 4], F32, tag="rc")
-                nc.vector.reciprocal(out=rc[:], in_=rsum[:])
-                osb = work.tile([P, 4, D], F32, tag="osb")
-                for w in range(4):
-                    nc.scalar.activation(out=osb[:, w, :], in_=po[:, w, :], func=ACT.Copy, scale=rc[:, w:w + 1])
-                nc.sync.dma_start(out=o_v[:, i - 3:i + 1, h * D:(h + 1) * D], in_=osb[:])
+        def stage_h(q4):
+            h, half = divmod(q4, 2)
+            rc = stat.tile([P, 4], F32, tag="rc")
+            nc.vector.reciprocal(out=rc[:], in_=st[("rs", q4)][:])
+            osb = work.tile([P, 4, D], F32, tag="osb")
+            nc.vector.tensor_tensor(
+                out=osb[:], in0=st[("po", q4)][:], in1=rc[:].unsqueeze(2).to_broadcast([P, 4, D]), op=ALU.mult
+            )
+            nc.sync.dma_start(out=o_v[:, 4 * half:4 * half + 4, h * D:(h + 1) * D], in_=osb[:])
 
+        for i0 in range(0, NT, 2):
+            nc.sync.dma_start(out=m_raw[:, i0:i0 + 2, :], in_=m_v[:, i0:i0 + 2, :])
         load_block(0)
-        load_mask(0, 2)
-        load_values(0)
-        load_mask(2, 4)
-        load_mask(4, 8)
         load_block(1)
-        load_values(1)
-        head_prep(0)
-        for h in range(H):
-            for i in range(NT):
-                if h == 0 and MASK_ON_PE:
-                    mask_prep(i)
-                unit(h, i)
-                if i == 0 and h % HB == 0 and 0 < h and h // HB + 1 < H // HB:
-                    load_block(h // HB + 1)
-                    load_values(h // HB + 1)
-                if i == 2 and h + 1 < H:
-                    head_prep(h + 1)
+        for i in range(NT):
+            mask_prep(i)
+        prep_transposes(0, 1)
+        prep_copy(0, 1)
+        prep_transposes(0, 0)
+        prep_copy(0, 0)
+        prep_regroup(0, False)
+        prep_quantise(0)
+
+        for k in range(N_UNITS + 7):
+            h, i = divmod(k, NT)
+            nxt = h + 1
+            if k - 6 >= 0 and (k - 6) % 4 == 3 and k - 6 < N_UNITS:
+                stage_h((k - 6) // 4)
+            if nxt < H and i == 2:
+                prep_copy(nxt, 1)
+            if nxt < H and i == 4:
+                prep_copy(nxt, 0)
+            if nxt < H and i == 6:
+                prep_quantise(nxt)
+            if k < N_UNITS:
+                stage_a(k)
+                stage_b(k, 0)
+            if 0 <= k - 4 < N_UNITS:
+                stage_f(k - 4)
+            if k < N_UNITS:
+                stage_b(k, 1)
+            if 0 <= k - 1 < N_UNITS:
+                stage_c(k - 1)
+            if 0 <= k - 2 < N_UNITS:
+                stage_d(k - 2)
+            if 0 <= k - 3 < N_UNITS:
+                stage_e(k - 3)
+            if 0 <= k - 5 < N_UNITS:
+                stage_g(k - 5)
+            if nxt < H and i == 1:
+                prep_transposes(nxt, 1)
+                prep_regroup(nxt, True)
+            if nxt < H and i == 3:
+                prep_transposes(nxt, 0)
+            if i == 0 and h % HB == 0 and 0 < h and h // HB + 1 < H // HB:
+                load_block(h // HB + 1)

@@ -17,15 +17,14 @@ S = 1024
 H = 16
 D = 128
 NT = S // P
-HB = 4
-CB = HB * D
 N_UNITS = H * NT
 FLOPS = 2 * 2 * H * S * S * D
 SQRT_D = math.sqrt(float(D))
 SCALE = 1.0 / SQRT_D
 
 PINNED = True
-E_ON_VECTOR_EVERY = 0
+E_ON_VECTOR_EVERY = 4
+MX_BATCH = 4
 
 
 def tile_flashattention_kernel(tc, query, key, value, attention_mask, out):
@@ -40,13 +39,14 @@ def tile_flashattention_kernel(tc, query, key, value, attention_mask, out):
         if PINNED:
             ctx.enter_context(tc.manual_schedule())
         const = ctx.enter_context(tc.tile_pool(name="const", bufs=1))
-        raw = ctx.enter_context(tc.tile_pool(name="raw", bufs=2))
+        raw = ctx.enter_context(tc.tile_pool(name="raw", bufs=3))
         hp = ctx.enter_context(tc.tile_pool(name="hp", bufs=2))
         work = ctx.enter_context(tc.tile_pool(name="work", bufs=3))
+        codes = ctx.enter_context(tc.tile_pool(name="codes", bufs=7))
         stat = ctx.enter_context(tc.tile_pool(name="stat", bufs=4))
         ps_sc = ctx.enter_context(tc.psum_pool(name="ps_sc", bufs=4))
-        ps_tr = ctx.enter_context(tc.psum_pool(name="ps_tr", bufs=2))
-        ps_o = ctx.enter_context(tc.psum_pool(name="ps_o", bufs=2))
+        ps_tr = ctx.enter_context(tc.psum_pool(name="ps_tr", bufs=3))
+        ps_o = ctx.enter_context(tc.psum_pool(name="ps_o", bufs=1))
 
         ident_bf = const.tile([P, P], BF16)
         make_identity(nc, ident_bf[:])
@@ -59,15 +59,19 @@ def tile_flashattention_kernel(tc, query, key, value, attention_mask, out):
         heads = {}
         st = {}
 
-        def load_block(cb):
-            cols = slice(cb * CB, (cb + 1) * CB)
-            kr = raw.tile([P, NT, CB], BF16, tag="kr")
+        def load_qk(h):
+            cols = slice(h * D, (h + 1) * D)
+            kr = raw.tile([P, NT, D], BF16, tag="kr")
             nc.sync.dma_start(out=kr[:], in_=k_v[:, :, cols])
-            qr = raw.tile([P, NT, CB], BF16, tag="qr")
+            qr = raw.tile([P, NT, D], BF16, tag="qr")
             nc.sync.dma_start(out=qr[:], in_=q_v[:, :, cols])
-            vr = raw.tile([P, NT, CB], BF16, tag="vr")
-            nc.sync.dma_start(out=vr[:], in_=v_v[:, :, cols])
-            blocks[cb] = (qr, kr, vr)
+            blocks[(h, 0)] = qr
+            blocks[(h, 1)] = kr
+
+        def load_v(h):
+            vr = raw.tile([P, NT, D], BF16, tag="vr")
+            nc.sync.dma_start(out=vr[:], in_=v_v[:, :, h * D:(h + 1) * D])
+            blocks[(h, 2)] = vr
 
         def mask_prep(i):
             tm = ps_sc.tile([P, NT, P], BF16, tag="sc")
@@ -79,11 +83,10 @@ def tile_flashattention_kernel(tc, query, key, value, attention_mask, out):
                 nc.vector.tensor_scalar(out=mask_t[:, i], in0=tm[:], scalar1=SQRT_D, scalar2=None, op0=ALU.mult)
 
         def prep_transposes(h, which):
-            cb, hc = divmod(h, HB)
-            src = blocks[cb][which]
+            src = blocks[(h, which)]
             tp = ps_sc.tile([P, NT, P], BF16, tag="sc")
             for j in range(NT):
-                nc.tensor.transpose(tp[:, j, :], src[:, j, hc * D:(hc + 1) * D], ident_bf[:])
+                nc.tensor.transpose(tp[:, j, :], src[:, j, :], ident_bf[:])
             st[("tp", h, which)] = tp
 
         def prep_copy(h, which):
@@ -93,10 +96,9 @@ def tile_flashattention_kernel(tc, query, key, value, attention_mask, out):
             heads[(h, which)] = x_t
 
         def prep_regroup(h, on_pool):
-            cb, hc = divmod(h, HB)
-            vr = blocks[cb][2]
+            vr = blocks[(h, 2)]
             gv = hp.tile([P, 2, D, 4], BF16, tag="gv", align_bytes=64)
-            v_src = vr[:, :, hc * D:(hc + 1) * D].rearrange("p (g t) c -> p g c t", g=2)
+            v_src = vr[:].rearrange("p (g t) c -> p g c t", g=2)
             if on_pool:
                 nc.gpsimd.tensor_scalar(out=gv[:], in0=v_src, scalar1=1.0, scalar2=0.0, op0=ALU.mult, op1=ALU.add)
             else:
@@ -166,7 +168,7 @@ def tile_flashattention_kernel(tc, query, key, value, attention_mask, out):
                 nc.tensor.transpose(te[:, b, :], e[:, b * P:(b + 1) * P], ident_bf[:])
 
         def e_on_vector(n):
-            return E_ON_VECTOR_EVERY > 0 and n % E_ON_VECTOR_EVERY == E_ON_VECTOR_EVERY - 1
+            return E_ON_VECTOR_EVERY > 0 and n % E_ON_VECTOR_EVERY == 0
 
         def stage_e(n):
             gr = work.tile([P, 2, P, 4], BF16, tag="gr", align_bytes=64)
@@ -178,8 +180,8 @@ def tile_flashattention_kernel(tc, query, key, value, attention_mask, out):
                 nc.scalar.copy(out=gr[:], in_=te_v)
 
         def stage_f(n):
-            cd = work.tile([P, 2 * P], U32, tag="cd", align_bytes=64)
-            sl = work.tile([P, 2 * P], U8, tag="sl", align_bytes=64)
+            cd = codes.tile([P, 2 * P], U32, tag="cd", align_bytes=64)
+            sl = codes.tile([P, 2 * P], U8, tag="sl", align_bytes=64)
             st[("cd", n)] = (cd, sl)
             nc.vector.quantize_mx(
                 out=cd[:].bitcast(FP8X4), scales=sl[:], in_=st[("gr", n)][:].rearrange("p g q t -> p (g q t)")
@@ -212,16 +214,19 @@ def tile_flashattention_kernel(tc, query, key, value, attention_mask, out):
             )
             nc.sync.dma_start(out=o_v[:, 4 * half:4 * half + 4, h * D:(h + 1) * D], in_=osb[:])
 
+        load_qk(0)
         for i0 in range(0, NT, 2):
             nc.sync.dma_start(out=m_raw[:, i0:i0 + 2, :], in_=m_v[:, i0:i0 + 2, :])
-        load_block(0)
-        load_block(1)
-        for i in range(NT):
-            mask_prep(i)
+        load_v(0)
+        for h in range(1, 3):
+            load_qk(h)
+            load_v(h)
         prep_transposes(0, 1)
         prep_copy(0, 1)
         prep_transposes(0, 0)
         prep_copy(0, 0)
+        for i in range(NT):
+            mask_prep(i)
         prep_regroup(0, False)
         prep_quantise(0)
 
@@ -236,6 +241,8 @@ def tile_flashattention_kernel(tc, query, key, value, attention_mask, out):
                 prep_copy(nxt, 0)
             if nxt < H and i == 6:
                 prep_quantise(nxt)
+            if 0 <= k - 3 < N_UNITS and e_on_vector(k - 3):
+                stage_e(k - 3)
             if k < N_UNITS:
                 stage_a(k)
                 stage_b(k, 0)
@@ -247,14 +254,16 @@ def tile_flashattention_kernel(tc, query, key, value, attention_mask, out):
                 stage_c(k - 1)
             if 0 <= k - 2 < N_UNITS:
                 stage_d(k - 2)
-            if 0 <= k - 3 < N_UNITS:
+            if 0 <= k - 3 < N_UNITS and not e_on_vector(k - 3):
                 stage_e(k - 3)
-            if 0 <= k - 5 < N_UNITS:
-                stage_g(k - 5)
+            if 0 <= k - 5 < N_UNITS and (k - 5) % MX_BATCH == MX_BATCH - 1:
+                for n in range(k - 4 - MX_BATCH, k - 4):
+                    stage_g(n)
             if nxt < H and i == 1:
                 prep_transposes(nxt, 1)
                 prep_regroup(nxt, True)
             if nxt < H and i == 3:
                 prep_transposes(nxt, 0)
-            if i == 0 and h % HB == 0 and 0 < h and h // HB + 1 < H // HB:
-                load_block(h // HB + 1)
+            if i == 0 and h + 3 < H:
+                load_qk(h + 3)
+                load_v(h + 3)

@@ -11,6 +11,7 @@ U8 = mybir.dt.uint8
 FP8X4 = mybir.dt.float8_e4m3fn_x4
 ALU = mybir.AluOpType
 ACT = mybir.ActivationFunctionType
+AX = mybir.AxisListType
 
 P = 128
 S = 1024
@@ -23,8 +24,10 @@ SQRT_D = math.sqrt(float(D))
 SCALE = 1.0 / SQRT_D
 
 PINNED = True
-E_ON_VECTOR_EVERY = 4
+E_ON_VECTOR_EVERY = 8
 MX_BATCH = 4
+V_ADD_EVERY = 8
+E_PHASE = 0
 
 
 def tile_flashattention_kernel(tc, query, key, value, attention_mask, out):
@@ -114,6 +117,9 @@ def tile_flashattention_kernel(tc, query, key, value, attention_mask, out):
             )
             heads[(h, 2)] = (vc, vs)
 
+        def v_adds(n):
+            return V_ADD_EVERY > 0 and n % V_ADD_EVERY == V_ADD_EVERY - 1
+
         def stage_a(n):
             h, i = divmod(n, NT)
             q_t = heads[(h, 0)]
@@ -123,8 +129,12 @@ def tile_flashattention_kernel(tc, query, key, value, attention_mask, out):
                 st[("sc", n, c)] = sc_c
                 nc.tensor.matmul(
                     sc_c[:], lhsT=q_t[:, i * P:(i + 1) * P], rhs=k_t[:, c * 512:(c + 1) * 512],
-                    start=True, stop=False,
+                    start=True, stop=v_adds(n),
                 )
+            if v_adds(n):
+                return
+            for c in range(2):
+                sc_c = st[("sc", n, c)]
                 for jj in range(4):
                     nc.tensor.matmul(
                         sc_c[:, jj * P:(jj + 1) * P], lhsT=mask_t[:, i, 4 * c + jj, :], rhs=ident_f[:],
@@ -135,12 +145,21 @@ def tile_flashattention_kernel(tc, query, key, value, attention_mask, out):
             if c == 0:
                 t_new = work.tile([P, S], F32, tag="t")
                 st[("t", n)] = t_new
-                nb0_new = stat.tile([P, 1], F32, tag="nb0")
-                st[("nb", n, 0)] = nb0_new
             else:
                 nb1_new = stat.tile([P, 1], F32, tag="nb1")
                 st[("nb", n, 1)] = nb1_new
             t = st[("t", n)]
+            if v_adds(n):
+                nc.vector.scalar_tensor_tensor(
+                    out=t[:, c * 512:(c + 1) * 512], in0=st[("sc", n, c)][:], scalar=-SCALE,
+                    in1=m_raw[:, n % NT, c * 512:(c + 1) * 512], op0=ALU.mult, op1=ALU.subtract,
+                )
+                if c == 1:
+                    nc.vector.tensor_reduce(out=st[("nb", n, 1)][:], in_=t[:], axis=AX.X, op=ALU.min)
+                return
+            if c == 0:
+                nb0_new = stat.tile([P, 1], F32, tag="nb0")
+                st[("nb", n, 0)] = nb0_new
             nc.vector.tensor_scalar(
                 out=t[:, c * 512:(c + 1) * 512], in0=st[("sc", n, c)][:], scalar1=-SCALE,
                 scalar2=(None if c == 0 else st[("nb", n, 0)][:]), op0=ALU.mult, op1=ALU.min,
@@ -168,7 +187,7 @@ def tile_flashattention_kernel(tc, query, key, value, attention_mask, out):
                 nc.tensor.transpose(te[:, b, :], e[:, b * P:(b + 1) * P], ident_bf[:])
 
         def e_on_vector(n):
-            return E_ON_VECTOR_EVERY > 0 and n % E_ON_VECTOR_EVERY == 0
+            return E_ON_VECTOR_EVERY > 0 and n % E_ON_VECTOR_EVERY == E_PHASE
 
         def stage_e(n):
             gr = work.tile([P, 2, P, 4], BF16, tag="gr", align_bytes=64)

@@ -26,7 +26,8 @@ SCALE = 1.0 / SQRT_D
 PINNED = True
 E_ON_VECTOR_EVERY = 8
 MX_BATCH = 4
-V_ADD_EVERY = 8
+MASK_AHEAD = 3
+V_ADD_EVERY = 0
 E_PHASE = 0
 
 
@@ -131,10 +132,8 @@ def tile_flashattention_kernel(tc, query, key, value, attention_mask, out):
                     sc_c[:], lhsT=q_t[:, i * P:(i + 1) * P], rhs=k_t[:, c * 512:(c + 1) * 512],
                     start=True, stop=v_adds(n),
                 )
-            if v_adds(n):
-                return
-            for c in range(2):
-                sc_c = st[("sc", n, c)]
+                if v_adds(n):
+                    continue
                 for jj in range(4):
                     nc.tensor.matmul(
                         sc_c[:, jj * P:(jj + 1) * P], lhsT=mask_t[:, i, 4 * c + jj, :], rhs=ident_f[:],
@@ -234,9 +233,10 @@ def tile_flashattention_kernel(tc, query, key, value, attention_mask, out):
             nc.sync.dma_start(out=o_v[:, 4 * half:4 * half + 4, h * D:(h + 1) * D], in_=osb[:])
 
         load_qk(0)
-        for i0 in range(0, NT, 2):
-            nc.sync.dma_start(out=m_raw[:, i0:i0 + 2, :], in_=m_v[:, i0:i0 + 2, :])
-        load_v(0)
+        for i in range(NT):
+            nc.sync.dma_start(out=m_raw[:, i:i + 1, :], in_=m_v[:, i:i + 1, :])
+            if i == MASK_AHEAD - 1:
+                load_v(0)
         for h in range(1, 3):
             load_qk(h)
             load_v(h)
@@ -244,7 +244,7 @@ def tile_flashattention_kernel(tc, query, key, value, attention_mask, out):
         prep_copy(0, 1)
         prep_transposes(0, 0)
         prep_copy(0, 0)
-        for i in range(NT):
+        for i in range(MASK_AHEAD):
             mask_prep(i)
         prep_regroup(0, False)
         prep_quantise(0)
@@ -273,6 +273,8 @@ def tile_flashattention_kernel(tc, query, key, value, attention_mask, out):
                 stage_c(k - 1)
             if 0 <= k - 2 < N_UNITS:
                 stage_d(k - 2)
+            if k + MASK_AHEAD < NT:
+                mask_prep(k + MASK_AHEAD)
             if 0 <= k - 3 < N_UNITS and not e_on_vector(k - 3):
                 stage_e(k - 3)
             if 0 <= k - 5 < N_UNITS and (k - 5) % MX_BATCH == MX_BATCH - 1:

@@ -24,7 +24,7 @@ SQRT_D = math.sqrt(float(D))
 SCALE = 1.0 / SQRT_D
 
 PINNED = True
-E_ON_VECTOR_EVERY = 8
+E_ON_VECTOR_EVERY = 0
 MX_BATCH = 4
 MASK_AHEAD = 3
 V_ADD_EVERY = 0
@@ -45,8 +45,10 @@ def tile_flashattention_kernel(tc, query, key, value, attention_mask, out):
         const = ctx.enter_context(tc.tile_pool(name="const", bufs=1))
         raw = ctx.enter_context(tc.tile_pool(name="raw", bufs=3))
         hp = ctx.enter_context(tc.tile_pool(name="hp", bufs=2))
-        work = ctx.enter_context(tc.tile_pool(name="work", bufs=3))
-        codes = ctx.enter_context(tc.tile_pool(name="codes", bufs=7))
+        work = ctx.enter_context(tc.tile_pool(name="work", bufs=4))
+        codes = ctx.enter_context(tc.tile_pool(name="codes", bufs=2))
+        xs = ctx.enter_context(tc.tile_pool(name="xs", bufs=6))
+        grp = ctx.enter_context(tc.tile_pool(name="grp", bufs=1))
         stat = ctx.enter_context(tc.tile_pool(name="stat", bufs=4))
         ps_sc = ctx.enter_context(tc.psum_pool(name="ps_sc", bufs=4))
         ps_tr = ctx.enter_context(tc.psum_pool(name="ps_tr", bufs=3))
@@ -99,14 +101,10 @@ def tile_flashattention_kernel(tc, query, key, value, attention_mask, out):
             nc.vector.tensor_copy(out=x_t[:], in_=tp[:].rearrange("p j q -> p (j q)"))
             heads[(h, which)] = x_t
 
-        def prep_regroup(h, on_pool):
+        def prep_regroup(h):
             vr = blocks[(h, 2)]
             gv = hp.tile([P, 2, D, 4], BF16, tag="gv", align_bytes=64)
-            v_src = vr[:].rearrange("p (g t) c -> p g c t", g=2)
-            if on_pool:
-                nc.gpsimd.tensor_scalar(out=gv[:], in0=v_src, scalar1=1.0, scalar2=0.0, op0=ALU.mult, op1=ALU.add)
-            else:
-                nc.vector.tensor_copy(out=gv[:], in_=v_src)
+            nc.scalar.copy(out=gv[:], in_=vr[:].rearrange("p (g t) c -> p g c t", g=2))
             st[("gv", h)] = gv
 
         def prep_quantise(h):
@@ -185,42 +183,46 @@ def tile_flashattention_kernel(tc, query, key, value, attention_mask, out):
             for b in range(NT):
                 nc.tensor.transpose(te[:, b, :], e[:, b * P:(b + 1) * P], ident_bf[:])
 
-        def e_on_vector(n):
-            return E_ON_VECTOR_EVERY > 0 and n % E_ON_VECTOR_EVERY == E_PHASE
-
         def stage_e(n):
-            gr = work.tile([P, 2, P, 4], BF16, tag="gr", align_bytes=64)
-            st[("gr", n)] = gr
-            te_v = st[("te", n)][:].rearrange("p (g t) q -> p g q t", g=2)
-            if e_on_vector(n):
-                nc.vector.tensor_copy(out=gr[:], in_=te_v)
-            else:
-                nc.scalar.copy(out=gr[:], in_=te_v)
+            x = xs.tile([P, NT, P], BF16, tag="x")
+            st[("x", n)] = x
+            nc.scalar.copy(out=x[:], in_=st[("te", n)][:])
 
-        def stage_f(n):
-            cd = codes.tile([P, 2 * P], U32, tag="cd", align_bytes=64)
-            sl = codes.tile([P, 2 * P], U8, tag="sl", align_bytes=64)
-            st[("cd", n)] = (cd, sl)
-            nc.vector.quantize_mx(
-                out=cd[:].bitcast(FP8X4), scales=sl[:], in_=st[("gr", n)][:].rearrange("p g q t -> p (g q t)")
-            )
-
-        def stage_g(n):
-            h = n // NT
+        def stage_p(n):
             u = n % 4
             if u == 0:
-                po_new = ps_o.tile([P, 4, D], F32, tag="po")
-                st[("po", n // 4)] = po_new
-            po = st[("po", n // 4)]
-            cd, sl = st[("cd", n)]
+                gr_new = grp.tile([P, 4, 2, P, 4], BF16, tag="gr", align_bytes=64)
+                st[("gr", n // 4)] = gr_new
+            gr = st[("gr", n // 4)]
+            nc.gpsimd.tensor_scalar(
+                out=gr[:, u], in0=st[("x", n)][:].rearrange("p (g t) q -> p g q t", g=2),
+                scalar1=1.0, scalar2=0.0, op0=ALU.mult, op1=ALU.add,
+            )
+
+        def stage_f(q4):
+            cd = codes.tile([P, 8 * P], U32, tag="cd", align_bytes=64)
+            sl = codes.tile([P, 8 * P], U8, tag="sl", align_bytes=64)
+            st[("cd", q4)] = (cd, sl)
+            nc.vector.quantize_mx(
+                out=cd[:].bitcast(FP8X4), scales=sl[:],
+                in_=st[("gr", q4)][:].rearrange("p u g q t -> p (u g q t)"),
+            )
+
+        def stage_g(q4):
+            h = q4 // 2
+            po = ps_o.tile([P, 4, D], F32, tag="po")
+            st[("po", q4)] = po
+            cd, sl = st[("cd", q4)]
             vc, vs = heads[(h, 2)]
-            for g in range(2):
-                nc.tensor.matmul_mx(
-                    out=po[:, u, :],
-                    lhsT=cd[:, g * P:(g + 1) * P].bitcast(FP8X4), lhsT_scale=sl[:, g * P:(g + 1) * P],
-                    rhs=vc[:, g * D:(g + 1) * D].bitcast(FP8X4), rhs_scale=vs[:, g * D:(g + 1) * D],
-                    start=(g == 0), stop=(g == 1),
-                )
+            for u in range(4):
+                for g in range(2):
+                    w = (2 * u + g) * P
+                    nc.tensor.matmul_mx(
+                        out=po[:, u, :],
+                        lhsT=cd[:, w:w + P].bitcast(FP8X4), lhsT_scale=sl[:, w:w + P],
+                        rhs=vc[:, g * D:(g + 1) * D].bitcast(FP8X4), rhs_scale=vs[:, g * D:(g + 1) * D],
+                        start=(g == 0), stop=(g == 1),
+                    )
 
         def stage_h(q4):
             h, half = divmod(q4, 2)
@@ -246,44 +248,43 @@ def tile_flashattention_kernel(tc, query, key, value, attention_mask, out):
         prep_copy(0, 0)
         for i in range(MASK_AHEAD):
             mask_prep(i)
-        prep_regroup(0, False)
+        prep_regroup(0)
         prep_quantise(0)
 
-        for k in range(N_UNITS + 7):
+        for k in range(N_UNITS + 12):
             h, i = divmod(k, NT)
             nxt = h + 1
-            if k - 6 >= 0 and (k - 6) % 4 == 3 and k - 6 < N_UNITS:
-                stage_h((k - 6) // 4)
-            if nxt < H and i == 2:
-                prep_copy(nxt, 1)
+            if k % 4 == 2 and 0 <= (k - 10) // 4 < N_UNITS // 4:
+                if i == 6 and 0 < h < H:
+                    prep_quantise(h)
+                stage_f((k - 10) // 4)
+            if k % 4 == 3 and 0 <= (k - 11) // 4 < N_UNITS // 4:
+                stage_h((k - 11) // 4)
             if nxt < H and i == 4:
+                prep_copy(nxt, 1)
+            if nxt < H and i == 5:
                 prep_copy(nxt, 0)
-            if nxt < H and i == 6:
-                prep_quantise(nxt)
-            if 0 <= k - 3 < N_UNITS and e_on_vector(k - 3):
-                stage_e(k - 3)
+            if 0 <= k - 4 < N_UNITS:
+                stage_e(k - 4)
             if k < N_UNITS:
                 stage_a(k)
                 stage_b(k, 0)
-            if 0 <= k - 4 < N_UNITS:
-                stage_f(k - 4)
-            if k < N_UNITS:
-                stage_b(k, 1)
             if 0 <= k - 1 < N_UNITS:
+                stage_b(k - 1, 1)
                 stage_c(k - 1)
-            if 0 <= k - 2 < N_UNITS:
-                stage_d(k - 2)
+            if 0 <= k - 3 < N_UNITS:
+                stage_d(k - 3)
             if k + MASK_AHEAD < NT:
                 mask_prep(k + MASK_AHEAD)
-            if 0 <= k - 3 < N_UNITS and not e_on_vector(k - 3):
-                stage_e(k - 3)
-            if 0 <= k - 5 < N_UNITS and (k - 5) % MX_BATCH == MX_BATCH - 1:
-                for n in range(k - 4 - MX_BATCH, k - 4):
-                    stage_g(n)
+            if 0 <= k - 5 < N_UNITS:
+                stage_p(k - 5)
+            if k % 4 == 2 and 0 <= (k - 10) // 4 < N_UNITS // 4:
+                stage_g((k - 10) // 4)
             if nxt < H and i == 1:
-                prep_transposes(nxt, 1)
-                prep_regroup(nxt, True)
+                prep_regroup(nxt)
             if nxt < H and i == 3:
+                prep_transposes(nxt, 1)
+            if nxt < H and i == 4:
                 prep_transposes(nxt, 0)
             if i == 0 and h + 3 < H:
                 load_qk(h + 3)

@@ -28,7 +28,7 @@ E_ON_VECTOR_EVERY = 0
 MX_BATCH = 4
 MASK_AHEAD = 3
 V_ADD_EVERY = 0
-E_PHASE = 0
+E_SKIP = 12
 
 
 def tile_flashattention_kernel(tc, query, key, value, attention_mask, out):
@@ -44,11 +44,10 @@ def tile_flashattention_kernel(tc, query, key, value, attention_mask, out):
             ctx.enter_context(tc.manual_schedule())
         const = ctx.enter_context(tc.tile_pool(name="const", bufs=1))
         raw = ctx.enter_context(tc.tile_pool(name="raw", bufs=3))
-        hp = ctx.enter_context(tc.tile_pool(name="hp", bufs=2))
+        hp = ctx.enter_context(tc.tile_pool(name="hp", bufs=3))
         work = ctx.enter_context(tc.tile_pool(name="work", bufs=4))
         codes = ctx.enter_context(tc.tile_pool(name="codes", bufs=2))
-        xs = ctx.enter_context(tc.tile_pool(name="xs", bufs=6))
-        grp = ctx.enter_context(tc.tile_pool(name="grp", bufs=1))
+        grp = ctx.enter_context(tc.tile_pool(name="grp", bufs=2))
         stat = ctx.enter_context(tc.tile_pool(name="stat", bufs=4))
         ps_sc = ctx.enter_context(tc.psum_pool(name="ps_sc", bufs=4))
         ps_tr = ctx.enter_context(tc.psum_pool(name="ps_tr", bufs=3))
@@ -104,7 +103,7 @@ def tile_flashattention_kernel(tc, query, key, value, attention_mask, out):
         def prep_regroup(h):
             vr = blocks[(h, 2)]
             gv = hp.tile([P, 2, D, 4], BF16, tag="gv", align_bytes=64)
-            nc.scalar.copy(out=gv[:], in_=vr[:].rearrange("p (g t) c -> p g c t", g=2))
+            nc.vector.tensor_copy(out=gv[:], in_=vr[:].rearrange("p (g t) c -> p g c t", g=2))
             st[("gv", h)] = gv
 
         def prep_quantise(h):
@@ -183,21 +182,20 @@ def tile_flashattention_kernel(tc, query, key, value, attention_mask, out):
             for b in range(NT):
                 nc.tensor.transpose(te[:, b, :], e[:, b * P:(b + 1) * P], ident_bf[:])
 
-        def stage_e(n):
-            x = xs.tile([P, NT, P], BF16, tag="x")
-            st[("x", n)] = x
-            nc.scalar.copy(out=x[:], in_=st[("te", n)][:])
+        def e_on_vector(n):
+            return n % 4 == 0 and n % 16 != E_SKIP
 
-        def stage_p(n):
+        def stage_e(n):
             u = n % 4
             if u == 0:
                 gr_new = grp.tile([P, 4, 2, P, 4], BF16, tag="gr", align_bytes=64)
                 st[("gr", n // 4)] = gr_new
             gr = st[("gr", n // 4)]
-            nc.gpsimd.tensor_scalar(
-                out=gr[:, u], in0=st[("x", n)][:].rearrange("p (g t) q -> p g q t", g=2),
-                scalar1=1.0, scalar2=0.0, op0=ALU.mult, op1=ALU.add,
-            )
+            te_v = st[("te", n)][:].rearrange("p (g t) q -> p g q t", g=2)
+            if e_on_vector(n):
+                nc.vector.tensor_copy(out=gr[:, u], in_=te_v)
+            else:
+                nc.scalar.copy(out=gr[:, u], in_=te_v)
 
         def stage_f(q4):
             cd = codes.tile([P, 8 * P], U32, tag="cd", align_bytes=64)
@@ -251,18 +249,19 @@ def tile_flashattention_kernel(tc, query, key, value, attention_mask, out):
         prep_regroup(0)
         prep_quantise(0)
 
-        for k in range(N_UNITS + 12):
+        for k in range(N_UNITS + 11):
             h, i = divmod(k, NT)
             nxt = h + 1
+            if k % 4 == 1 and 0 <= (k - 9) // 4 < N_UNITS // 4:
+                stage_f((k - 9) // 4)
             if k % 4 == 2 and 0 <= (k - 10) // 4 < N_UNITS // 4:
-                if i == 6 and 0 < h < H:
-                    prep_quantise(h)
-                stage_f((k - 10) // 4)
-            if k % 4 == 3 and 0 <= (k - 11) // 4 < N_UNITS // 4:
-                stage_h((k - 11) // 4)
-            if nxt < H and i == 4:
+                stage_h((k - 10) // 4)
+            if nxt < H and i == 6:
+                prep_regroup(nxt)
+                prep_quantise(nxt)
+            if nxt < H and i == 3:
                 prep_copy(nxt, 1)
-            if nxt < H and i == 5:
+            if nxt < H and i == 7:
                 prep_copy(nxt, 0)
             if 0 <= k - 4 < N_UNITS:
                 stage_e(k - 4)
@@ -276,15 +275,11 @@ def tile_flashattention_kernel(tc, query, key, value, attention_mask, out):
                 stage_d(k - 3)
             if k + MASK_AHEAD < NT:
                 mask_prep(k + MASK_AHEAD)
-            if 0 <= k - 5 < N_UNITS:
-                stage_p(k - 5)
-            if k % 4 == 2 and 0 <= (k - 10) // 4 < N_UNITS // 4:
-                stage_g((k - 10) // 4)
-            if nxt < H and i == 1:
-                prep_regroup(nxt)
-            if nxt < H and i == 3:
+            if k % 4 == 1 and 0 <= (k - 9) // 4 < N_UNITS // 4:
+                stage_g((k - 9) // 4)
+            if nxt < H and i == 2:
                 prep_transposes(nxt, 1)
-            if nxt < H and i == 4:
+            if nxt < H and i == 6:
                 prep_transposes(nxt, 0)
             if i == 0 and h + 3 < H:
                 load_qk(h + 3)

@@ -24,11 +24,11 @@ SQRT_D = math.sqrt(float(D))
 SCALE = 1.0 / SQRT_D
 
 PINNED = True
-E_ON_VECTOR_EVERY = 0
+E_ON_VECTOR_EVERY = 8
 MX_BATCH = 4
-MASK_AHEAD = 3
+MASK_AHEAD = 2
 V_ADD_EVERY = 0
-E_SKIP = 12
+E_PHASE = 0
 
 
 def tile_flashattention_kernel(tc, query, key, value, attention_mask, out):
@@ -44,10 +44,10 @@ def tile_flashattention_kernel(tc, query, key, value, attention_mask, out):
             ctx.enter_context(tc.manual_schedule())
         const = ctx.enter_context(tc.tile_pool(name="const", bufs=1))
         raw = ctx.enter_context(tc.tile_pool(name="raw", bufs=3))
-        hp = ctx.enter_context(tc.tile_pool(name="hp", bufs=3))
-        work = ctx.enter_context(tc.tile_pool(name="work", bufs=4))
-        codes = ctx.enter_context(tc.tile_pool(name="codes", bufs=2))
-        grp = ctx.enter_context(tc.tile_pool(name="grp", bufs=2))
+        hp = ctx.enter_context(tc.tile_pool(name="hp", bufs=2))
+        work = ctx.enter_context(tc.tile_pool(name="work", bufs=3))
+        codes = ctx.enter_context(tc.tile_pool(name="codes", bufs=7))
+        ring = ctx.enter_context(tc.tile_pool(name="ring", bufs=4))
         stat = ctx.enter_context(tc.tile_pool(name="stat", bufs=4))
         ps_sc = ctx.enter_context(tc.psum_pool(name="ps_sc", bufs=4))
         ps_tr = ctx.enter_context(tc.psum_pool(name="ps_tr", bufs=3))
@@ -100,10 +100,14 @@ def tile_flashattention_kernel(tc, query, key, value, attention_mask, out):
             nc.vector.tensor_copy(out=x_t[:], in_=tp[:].rearrange("p j q -> p (j q)"))
             heads[(h, which)] = x_t
 
-        def prep_regroup(h):
+        def prep_regroup(h, on_pool):
             vr = blocks[(h, 2)]
-            gv = hp.tile([P, 2, D, 4], BF16, tag="gv", align_bytes=64)
-            nc.vector.tensor_copy(out=gv[:], in_=vr[:].rearrange("p (g t) c -> p g c t", g=2))
+            gv = ring.tile([P, 2, D, 4], BF16, tag="gr", align_bytes=64)
+            v_src = vr[:].rearrange("p (g t) c -> p g c t", g=2)
+            if on_pool:
+                nc.gpsimd.tensor_scalar(out=gv[:], in0=v_src, scalar1=1.0, scalar2=0.0, op0=ALU.mult, op1=ALU.add)
+            else:
+                nc.vector.tensor_copy(out=gv[:], in_=v_src)
             st[("gv", h)] = gv
 
         def prep_quantise(h):
@@ -183,44 +187,41 @@ def tile_flashattention_kernel(tc, query, key, value, attention_mask, out):
                 nc.tensor.transpose(te[:, b, :], e[:, b * P:(b + 1) * P], ident_bf[:])
 
         def e_on_vector(n):
-            return n % 4 == 0 and n % 16 != E_SKIP
+            return n % 8 == 0 or n % 32 == 4
 
         def stage_e(n):
-            u = n % 4
-            if u == 0:
-                gr_new = grp.tile([P, 4, 2, P, 4], BF16, tag="gr", align_bytes=64)
-                st[("gr", n // 4)] = gr_new
-            gr = st[("gr", n // 4)]
+            gr = ring.tile([P, 2, P, 4], BF16, tag="gr", align_bytes=64)
+            st[("gr", n)] = gr
             te_v = st[("te", n)][:].rearrange("p (g t) q -> p g q t", g=2)
             if e_on_vector(n):
-                nc.vector.tensor_copy(out=gr[:, u], in_=te_v)
+                nc.vector.tensor_copy(out=gr[:], in_=te_v)
             else:
-                nc.scalar.copy(out=gr[:, u], in_=te_v)
+                nc.scalar.copy(out=gr[:], in_=te_v)
 
-        def stage_f(q4):
-            cd = codes.tile([P, 8 * P], U32, tag="cd", align_bytes=64)
-            sl = codes.tile([P, 8 * P], U8, tag="sl", align_bytes=64)
-            st[("cd", q4)] = (cd, sl)
+        def stage_f(n):
+            cd = codes.tile([P, 2 * P], U32, tag="cd", align_bytes=64)
+            sl = codes.tile([P, 2 * P], U8, tag="sl", align_bytes=64)
+            st[("cd", n)] = (cd, sl)
             nc.vector.quantize_mx(
-                out=cd[:].bitcast(FP8X4), scales=sl[:],
-                in_=st[("gr", q4)][:].rearrange("p u g q t -> p (u g q t)"),
+                out=cd[:].bitcast(FP8X4), scales=sl[:], in_=st[("gr", n)][:].rearrange("p g q t -> p (g q t)")
             )
 
-        def stage_g(q4):
-            h = q4 // 2
-            po = ps_o.tile([P, 4, D], F32, tag="po")
-            st[("po", q4)] = po
-            cd, sl = st[("cd", q4)]
+        def stage_g(n):
+            h = n // NT
+            u = n % 4
+            if u == 0:
+                po_new = ps_o.tile([P, 4, D], F32, tag="po")
+                st[("po", n // 4)] = po_new
+            po = st[("po", n // 4)]
+            cd, sl = st[("cd", n)]
             vc, vs = heads[(h, 2)]
-            for u in range(4):
-                for g in range(2):
-                    w = (2 * u + g) * P
-                    nc.tensor.matmul_mx(
-                        out=po[:, u, :],
-                        lhsT=cd[:, w:w + P].bitcast(FP8X4), lhsT_scale=sl[:, w:w + P],
-                        rhs=vc[:, g * D:(g + 1) * D].bitcast(FP8X4), rhs_scale=vs[:, g * D:(g + 1) * D],
-                        start=(g == 0), stop=(g == 1),
-                    )
+            for g in range(2):
+                nc.tensor.matmul_mx(
+                    out=po[:, u, :],
+                    lhsT=cd[:, g * P:(g + 1) * P].bitcast(FP8X4), lhsT_scale=sl[:, g * P:(g + 1) * P],
+                    rhs=vc[:, g * D:(g + 1) * D].bitcast(FP8X4), rhs_scale=vs[:, g * D:(g + 1) * D],
+                    start=(g == 0), stop=(g == 1),
+                )
 
         def stage_h(q4):
             h, half = divmod(q4, 2)
@@ -246,40 +247,45 @@ def tile_flashattention_kernel(tc, query, key, value, attention_mask, out):
         prep_copy(0, 0)
         for i in range(MASK_AHEAD):
             mask_prep(i)
-        prep_regroup(0)
+        prep_regroup(0, False)
         prep_quantise(0)
 
-        for k in range(N_UNITS + 11):
+        for k in range(N_UNITS + 7):
             h, i = divmod(k, NT)
             nxt = h + 1
-            if k % 4 == 1 and 0 <= (k - 9) // 4 < N_UNITS // 4:
-                stage_f((k - 9) // 4)
-            if k % 4 == 2 and 0 <= (k - 10) // 4 < N_UNITS // 4:
-                stage_h((k - 10) // 4)
-            if nxt < H and i == 6:
-                prep_regroup(nxt)
-                prep_quantise(nxt)
-            if nxt < H and i == 3:
+            if k - 6 >= 0 and (k - 6) % 4 == 3 and k - 6 < N_UNITS:
+                stage_h((k - 6) // 4)
+            if nxt < H and i == 2:
                 prep_copy(nxt, 1)
-            if nxt < H and i == 7:
+            if nxt < H and i == 4:
                 prep_copy(nxt, 0)
-            if 0 <= k - 4 < N_UNITS:
-                stage_e(k - 4)
+            if nxt < H and i == 6:
+                prep_quantise(nxt)
+            if 0 <= k - 3 < N_UNITS and e_on_vector(k - 3):
+                stage_e(k - 3)
             if k < N_UNITS:
                 stage_a(k)
                 stage_b(k, 0)
+            if 0 <= k - 4 < N_UNITS:
+                stage_f(k - 4)
+            if k < N_UNITS:
+                stage_b(k, 1)
             if 0 <= k - 1 < N_UNITS:
-                stage_b(k - 1, 1)
                 stage_c(k - 1)
-            if 0 <= k - 3 < N_UNITS:
-                stage_d(k - 3)
+            if 0 <= k - 2 < N_UNITS:
+                stage_d(k - 2)
             if k + MASK_AHEAD < NT:
                 mask_prep(k + MASK_AHEAD)
-            if k % 4 == 1 and 0 <= (k - 9) // 4 < N_UNITS // 4:
-                stage_g((k - 9) // 4)
-            if nxt < H and i == 2:
+            if 0 <= k - 3 < N_UNITS and not e_on_vector(k - 3):
+                stage_e(k - 3)
+            if 0 <= k - 5 < N_UNITS and (k - 5) % MX_BATCH == MX_BATCH - 1:
+                for n in range(k - 4 - MX_BATCH, k - 4):
+                    stage_g(n)
+            if nxt < H and i == 1:
                 prep_transposes(nxt, 1)
-            if nxt < H and i == 6:
+            if nxt < H and i == 4:
+                prep_regroup(nxt, True)
+            if nxt < H and i == 3:
                 prep_transposes(nxt, 0)
             if i == 0 and h + 3 < H:
                 load_qk(h + 3)

import math
from contextlib import ExitStack

import concourse.mybir as mybir
from concourse.masks import make_identity

F32 = mybir.dt.float32
BF16 = mybir.dt.bfloat16
U32 = mybir.dt.uint32
U8 = mybir.dt.uint8
FP8X4 = mybir.dt.float8_e4m3fn_x4
ALU = mybir.AluOpType
ACT = mybir.ActivationFunctionType
AX = mybir.AxisListType

P = 128
S = 1024
H = 16
D = 128
NT = S // P
N_UNITS = H * NT
FLOPS = 2 * 2 * H * S * S * D
SQRT_D = math.sqrt(float(D))
SCALE = 1.0 / SQRT_D

PINNED = True
E_ON_VECTOR_EVERY = 8
MX_BATCH = 4
MASK_AHEAD = 2
V_ADD_EVERY = 0
E_PHASE = 0


def tile_flashattention_kernel(tc, query, key, value, attention_mask, out):
    nc = tc.nc
    q_v = query.rearrange("b (i p) c -> p (b i) c", p=P)
    k_v = key.rearrange("b (i p) c -> p (b i) c", p=P)
    v_v = value.rearrange("b (i p) c -> p (b i) c", p=P)
    m_v = attention_mask.rearrange("a b (i p) k -> p (a b i) k", p=P)
    o_v = out.rearrange("b (i p) c -> p (b i) c", p=P)

    with ExitStack() as ctx:
        if PINNED:
            ctx.enter_context(tc.manual_schedule())
        const = ctx.enter_context(tc.tile_pool(name="const", bufs=1))
        raw = ctx.enter_context(tc.tile_pool(name="raw", bufs=3))
        hp = ctx.enter_context(tc.tile_pool(name="hp", bufs=2))
        work = ctx.enter_context(tc.tile_pool(name="work", bufs=3))
        codes = ctx.enter_context(tc.tile_pool(name="codes", bufs=7))
        ring = ctx.enter_context(tc.tile_pool(name="ring", bufs=4))
        stat = ctx.enter_context(tc.tile_pool(name="stat", bufs=4))
        ps_sc = ctx.enter_context(tc.psum_pool(name="ps_sc", bufs=4))
        ps_tr = ctx.enter_context(tc.psum_pool(name="ps_tr", bufs=3))
        ps_o = ctx.enter_context(tc.psum_pool(name="ps_o", bufs=1))

        ident_bf = const.tile([P, P], BF16)
        make_identity(nc, ident_bf[:])
        ident_f = const.tile([P, P], F32)
        make_identity(nc, ident_f[:])
        m_raw = const.tile([P, NT, S], BF16)
        mask_t = const.tile([P, NT, NT, P], F32)

        blocks = {}
        heads = {}
        st = {}

        def load_qk(h):
            cols = slice(h * D, (h + 1) * D)
            kr = raw.tile([P, NT, D], BF16, tag="kr")
            nc.sync.dma_start(out=kr[:], in_=k_v[:, :, cols])
            qr = raw.tile([P, NT, D], BF16, tag="qr")
            nc.sync.dma_start(out=qr[:], in_=q_v[:, :, cols])
            blocks[(h, 0)] = qr
            blocks[(h, 1)] = kr

        def load_v(h):
            vr = raw.tile([P, NT, D], BF16, tag="vr")
            nc.sync.dma_start(out=vr[:], in_=v_v[:, :, h * D:(h + 1) * D])
            blocks[(h, 2)] = vr

        def mask_prep(i):
            tm = ps_sc.tile([P, NT, P], BF16, tag="sc")
            for j in range(NT):
                nc.tensor.transpose(tm[:, j, :], m_raw[:, i, j * P:(j + 1) * P], ident_bf[:])
            if i % 2 == 0:
                nc.scalar.activation(out=mask_t[:, i], in_=tm[:], func=ACT.Copy, scale=SQRT_D)
            else:
                nc.vector.tensor_scalar(out=mask_t[:, i], in0=tm[:], scalar1=SQRT_D, scalar2=None, op0=ALU.mult)

        def prep_transposes(h, which):
            src = blocks[(h, which)]
            tp = ps_sc.tile([P, NT, P], BF16, tag="sc")
            for j in range(NT):
                nc.tensor.transpose(tp[:, j, :], src[:, j, :], ident_bf[:])
            st[("tp", h, which)] = tp

        def prep_copy(h, which):
            tp = st[("tp", h, which)]
            x_t = hp.tile([P, S], BF16, tag="x_t%d" % which)
            nc.vector.tensor_copy(out=x_t[:], in_=tp[:].rearrange("p j q -> p (j q)"))
            heads[(h, which)] = x_t

        def prep_regroup(h, on_pool):
            vr = blocks[(h, 2)]
            gv = ring.tile([P, 2, D, 4], BF16, tag="gr", align_bytes=64)
            v_src = vr[:].rearrange("p (g t) c -> p g c t", g=2)
            if on_pool:
                nc.gpsimd.tensor_scalar(out=gv[:], in0=v_src, scalar1=1.0, scalar2=0.0, op0=ALU.mult, op1=ALU.add)
            else:
                nc.vector.tensor_copy(out=gv[:], in_=v_src)
            st[("gv", h)] = gv

        def prep_quantise(h):
            gv = st[("gv", h)]
            vc = hp.tile([P, 2 * D], U32, tag="vc", align_bytes=64)
            vs = hp.tile([P, 2 * D], U8, tag="vs", align_bytes=64)
            nc.vector.quantize_mx(
                out=vc[:].bitcast(FP8X4), scales=vs[:], in_=gv[:].rearrange("p g c t -> p (g c t)")
            )
            heads[(h, 2)] = (vc, vs)

        def v_adds(n):
            return V_ADD_EVERY > 0 and n % V_ADD_EVERY == V_ADD_EVERY - 1

        def stage_a(n):
            h, i = divmod(n, NT)
            q_t = heads[(h, 0)]
            k_t = heads[(h, 1)]
            for c in range(2):
                sc_c = ps_sc.tile([P, 512], F32, tag="sc")
                st[("sc", n, c)] = sc_c
                nc.tensor.matmul(
                    sc_c[:], lhsT=q_t[:, i * P:(i + 1) * P], rhs=k_t[:, c * 512:(c + 1) * 512],
                    start=True, stop=v_adds(n),
                )
                if v_adds(n):
                    continue
                for jj in range(4):
                    nc.tensor.matmul(
                        sc_c[:, jj * P:(jj + 1) * P], lhsT=mask_t[:, i, 4 * c + jj, :], rhs=ident_f[:],
                        is_transpose=True, start=False, stop=(jj == 3),
                    )

        def stage_b(n, c):
            if c == 0:
                t_new = work.tile([P, S], F32, tag="t")
                st[("t", n)] = t_new
            else:
                nb1_new = stat.tile([P, 1], F32, tag="nb1")
                st[("nb", n, 1)] = nb1_new
            t = st[("t", n)]
            if v_adds(n):
                nc.vector.scalar_tensor_tensor(
                    out=t[:, c * 512:(c + 1) * 512], in0=st[("sc", n, c)][:], scalar=-SCALE,
                    in1=m_raw[:, n % NT, c * 512:(c + 1) * 512], op0=ALU.mult, op1=ALU.subtract,
                )
                if c == 1:
                    nc.vector.tensor_reduce(out=st[("nb", n, 1)][:], in_=t[:], axis=AX.X, op=ALU.min)
                return
            if c == 0:
                nb0_new = stat.tile([P, 1], F32, tag="nb0")
                st[("nb", n, 0)] = nb0_new
            nc.vector.tensor_scalar(
                out=t[:, c * 512:(c + 1) * 512], in0=st[("sc", n, c)][:], scalar1=-SCALE,
                scalar2=(None if c == 0 else st[("nb", n, 0)][:]), op0=ALU.mult, op1=ALU.min,
                accum_out=st[("nb", n, c)][:],
            )

        def stage_c(n):
            u = n % 4
            if u == 0:
                rs_new = stat.tile([P, 4], F32, tag="rs")
                st[("rs", n // 4)] = rs_new
            rs = st[("rs", n // 4)]
            e = work.tile([P, S], BF16, tag="e")
            st[("e", n)] = e
            nc.scalar.activation(
                out=e[:], in_=st[("t", n)][:], func=ACT.Exp, bias=st[("nb", n, 1)][:], scale=-1.0,
                accum_out=rs[:, u:u + 1],
            )

        def stage_d(n):
            e = st[("e", n)]
            te = ps_tr.tile([P, NT, P], BF16, tag="tr")
            st[("te", n)] = te
            for b in range(NT):
                nc.tensor.transpose(te[:, b, :], e[:, b * P:(b + 1) * P], ident_bf[:])

        def e_on_vector(n):
            return n % 8 == 0 or n % 32 == 4

        def stage_e(n):
            gr = ring.tile([P, 2, P, 4], BF16, tag="gr", align_bytes=64)
            st[("gr", n)] = gr
            te_v = st[("te", n)][:].rearrange("p (g t) q -> p g q t", g=2)
            if e_on_vector(n):
                nc.vector.tensor_copy(out=gr[:], in_=te_v)
            else:
                nc.scalar.copy(out=gr[:], in_=te_v)

        def stage_f(n):
            cd = codes.tile([P, 2 * P], U32, tag="cd", align_bytes=64)
            sl = codes.tile([P, 2 * P], U8, tag="sl", align_bytes=64)
            st[("cd", n)] = (cd, sl)
            nc.vector.quantize_mx(
                out=cd[:].bitcast(FP8X4), scales=sl[:], in_=st[("gr", n)][:].rearrange("p g q t -> p (g q t)")
            )

        def stage_g(n):
            h = n // NT
            u = n % 4
            if u == 0:
                po_new = ps_o.tile([P, 4, D], F32, tag="po")
                st[("po", n // 4)] = po_new
            po = st[("po", n // 4)]
            cd, sl = st[("cd", n)]
            vc, vs = heads[(h, 2)]
            for g in range(2):
                nc.tensor.matmul_mx(
                    out=po[:, u, :],
                    lhsT=cd[:, g * P:(g + 1) * P].bitcast(FP8X4), lhsT_scale=sl[:, g * P:(g + 1) * P],
                    rhs=vc[:, g * D:(g + 1) * D].bitcast(FP8X4), rhs_scale=vs[:, g * D:(g + 1) * D],
                    start=(g == 0), stop=(g == 1),
                )

        def stage_h(q4):
            h, half = divmod(q4, 2)
            rc = stat.tile([P, 4], F32, tag="rc")
            nc.vector.reciprocal(out=rc[:], in_=st[("rs", q4)][:])
            osb = work.tile([P, 4, D], F32, tag="osb")
            nc.vector.tensor_tensor(
                out=osb[:], in0=st[("po", q4)][:], in1=rc[:].unsqueeze(2).to_broadcast([P, 4, D]), op=ALU.mult
            )
            nc.sync.dma_start(out=o_v[:, 4 * half:4 * half + 4, h * D:(h + 1) * D], in_=osb[:])

        load_qk(0)
        for i in range(NT):
            nc.sync.dma_start(out=m_raw[:, i:i + 1, :], in_=m_v[:, i:i + 1, :])
            if i == MASK_AHEAD - 1:
                load_v(0)
        for h in range(1, 3):
            load_qk(h)
            load_v(h)
        prep_transposes(0, 1)
        prep_copy(0, 1)
        prep_transposes(0, 0)
        prep_copy(0, 0)
        for i in range(MASK_AHEAD):
            mask_prep(i)
        prep_regroup(0, False)
        prep_quantise(0)

        for k in range(N_UNITS + 7):
            h, i = divmod(k, NT)
            nxt = h + 1
            if k - 6 >= 0 and (k - 6) % 4 == 3 and k - 6 < N_UNITS:
                stage_h((k - 6) // 4)
            if nxt < H and i == 2:
                prep_copy(nxt, 1)
            if nxt < H and i == 4:
                prep_copy(nxt, 0)
            if nxt < H and i == 6:
                prep_quantise(nxt)
            if 0 <= k - 3 < N_UNITS and e_on_vector(k - 3):
                stage_e(k - 3)
            if k < N_UNITS:
                stage_a(k)
                stage_b(k, 0)
            if 0 <= k - 4 < N_UNITS:
                stage_f(k - 4)
            if k < N_UNITS:
                stage_b(k, 1)
            if 0 <= k - 1 < N_UNITS:
                stage_c(k - 1)
            if 0 <= k - 2 < N_UNITS:
                stage_d(k - 2)
            if k + MASK_AHEAD < NT:
                mask_prep(k + MASK_AHEAD)
            if 0 <= k - 3 < N_UNITS and not e_on_vector(k - 3):
                stage_e(k - 3)
            if 0 <= k - 5 < N_UNITS and (k - 5) % MX_BATCH == MX_BATCH - 1:
                for n in range(k - 4 - MX_BATCH, k - 4):
                    stage_g(n)
            if nxt < H and i == 1:
                prep_transposes(nxt, 1)
            if nxt < H and i == 4:
                prep_regroup(nxt, True)
            if nxt < H and i == 3:
                prep_transposes(nxt, 0)
            if i == 0 and h + 3 < H:
                load_qk(h + 3)
                load_v(h + 3)
